import numpy as np
import ml_dtypes

BF16 = ml_dtypes.bfloat16


def bf(x):
    return np.asarray(x, np.float32).astype(BF16)


def f32(x):
    return np.asarray(x, np.float32)


def f64(x):
    return np.asarray(x).astype(np.float64)


def striped(idx):
    return np.tile(idx.reshape(-1, 16).T, (8, 1))


K, S, N, T, F = 256, 1024, 512, 128, 2
OFF = 0.5


def setup_inputs():
    return {"x": bf((np.random.standard_normal((F, T, N)) + OFF) / np.sqrt(T)), "clusters": bf((np.random.standard_normal((F, T, K)) + OFF) / np.sqrt(T)), "base": f32(3.0 + 0.5 * np.random.standard_normal((K, S))), "offs": striped(np.random.permutation(S)[:N])}


def reference(x, clusters, base, offs):
    idx = offs[:16].T.reshape(-1)
    xs, cs = f64(x), f64(clusters)
    parts = []
    for f in range(F):
        x2 = (xs[f] * xs[f]).sum(axis=0)[None, :]
        c2 = (cs[f] * cs[f]).sum(axis=0)[:, None]
        xc = cs[f].T @ xs[f]
        parts.append(np.sqrt(np.maximum(x2 + c2 - 2.0 * xc, 0.0)))
    out = f64(base).copy()
    out[:, idx] = parts[0] + parts[1]
    return out

@@ -1,0 +1,62 @@
+import concourse.mybir as mybir
+
+F, T, N = 2, 128, 512
+K, S = 256, 1024
+P = 128
+BLOCKS = K // P
+
+BF16, F32, U16 = mybir.dt.bfloat16, mybir.dt.float32, mybir.dt.uint16
+ALU = mybir.AluOpType
+ACT = mybir.ActivationFunctionType
+
+FLOPS = 2 * F * T * K * N
+
+
+def tile_softkmeans_kernel(tc, x, clusters, base, offs, out):
+    nc = tc.nc
+    with (
+        tc.tile_pool(name="held", bufs=1) as held,
+        tc.tile_pool(name="work", bufs=2) as work,
+        tc.psum_pool(name="psum", bufs=BLOCKS * F) as psum,
+    ):
+        offsets = held.tile([P, N // 16], U16, name="offsets")
+        nc.sync.dma_start(offsets[:], offs)
+        c_all = held.tile([T, F, K], BF16, name="c_all")
+        nc.scalar.dma_start(c_all[:], clusters.rearrange("f t k -> t f k"))
+        x_of = [held.tile([T, N], BF16, name=f"x{f}") for f in range(F)]
+        for f in range(F):
+            nc.sync.dma_start(x_of[f][:], x[f])
+        window_of = [held.tile([P, S], F32, name=f"window{b}") for b in range(BLOCKS)]
+        for b in range(BLOCKS):
+            nc.gpsimd.dma_start(window_of[b][:], base[b * P : (b + 1) * P, :])
+
+        minus_half = held.tile([T, N], BF16, name="minus_half")
+        nc.vector.memset(minus_half[:], -0.5)
+        c_squared = held.tile([T, F, K], BF16, name="c_squared")
+        nc.vector.tensor_mul(c_squared[:], c_all[:], c_all[:])
+        x_squared_of = [held.tile([T, N], BF16, name=f"x_squared{f}") for f in range(F)]
+        for f in range(F):
+            nc.vector.tensor_mul(x_squared_of[f][:], x_of[f][:], x_of[f][:])
+
+        for b in range(BLOCKS):
+            block = slice(b * P, (b + 1) * P)
+            root_of = []
+            for f in range(F):
+                acc = psum.tile([P, N], F32, name="acc")
+                nc.tensor.matmul(acc[:], c_squared[:, f, block], minus_half[:], start=True, stop=False)
+                nc.tensor.matmul(acc[:], c_all[:, f, block], x_of[f][:], start=False, stop=False)
+                nc.tensor.matmul(acc[:], minus_half[:, 0:P], x_squared_of[f][:], start=False, stop=True)
+
+                d2 = work.tile([P, N], F32, name=f"d2_{f}")
+                if b == 0:
+                    nc.vector.tensor_scalar(d2[:], acc[:], -2.0, 0.0, ALU.mult, ALU.max)
+                else:
+                    nc.scalar.activation(d2[:], acc[:], ACT.Relu, scale=-2.0)
+                root = work.tile([P, N], F32, name=f"root{f}")
+                nc.scalar.activation(root[:], d2[:], ACT.Sqrt)
+                root_of.append(root)
+
+            nc.vector.tensor_tensor(
+                window_of[b][:].indirect(offsets[:]), root_of[0][:], root_of[1][:], ALU.add
+            )
+            nc.sync.dma_start(out[block, :], window_of[b][:])

@@ -4,6 +4,7 @@ F, T, N = 2, 128, 512
 K, S = 256, 1024
 P = 128
 BLOCKS = K // P
+WARM_UP_MATMULS = 16
 
 BF16, F32, U16 = mybir.dt.bfloat16, mybir.dt.float32, mybir.dt.uint16
 ALU = mybir.AluOpType
@@ -18,17 +19,24 @@ def tile_softkmeans_kernel(tc, x, clusters, base, offs, out):
         tc.tile_pool(name="held", bufs=1) as held,
         tc.tile_pool(name="work", bufs=2) as work,
         tc.psum_pool(name="psum", bufs=BLOCKS * F) as psum,
+        tc.psum_pool(name="psum_warm", bufs=1) as psum_warm,
     ):
-        offsets = held.tile([P, N // 16], U16, name="offsets")
-        nc.sync.dma_start(offsets[:], offs)
+        zeros = held.tile([P, P], BF16, name="zeros")
+        nc.gpsimd.memset(zeros[:], 0.0)
+        warm_up = psum_warm.tile([P, P], F32, name="warm_up")
+        for i in range(WARM_UP_MATMULS):
+            nc.tensor.matmul(warm_up[:], zeros[:], zeros[:], start=True, stop=True)
+
         c_all = held.tile([T, F, K], BF16, name="c_all")
-        nc.scalar.dma_start(c_all[:], clusters.rearrange("f t k -> t f k"))
+        nc.sync.dma_start(c_all[:], clusters.rearrange("f t k -> t f k"))
         x_of = [held.tile([T, N], BF16, name=f"x{f}") for f in range(F)]
         for f in range(F):
             nc.sync.dma_start(x_of[f][:], x[f])
+        offsets = held.tile([P, N // 16], U16, name="offsets")
+        nc.sync.dma_start(offsets[:], offs)
         window_of = [held.tile([P, S], F32, name=f"window{b}") for b in range(BLOCKS)]
         for b in range(BLOCKS):
-            nc.gpsimd.dma_start(window_of[b][:], base[b * P : (b + 1) * P, :])
+            nc.sync.dma_start(window_of[b][:], base[b * P : (b + 1) * P, :])
 
         minus_half = held.tile([T, N], BF16, name="minus_half")
         nc.vector.memset(minus_half[:], -0.5)
@@ -43,8 +51,8 @@ def tile_softkmeans_kernel(tc, x, clusters, base, offs, out):
             root_of = []
             for f in range(F):
                 acc = psum.tile([P, N], F32, name="acc")
-                nc.tensor.matmul(acc[:], c_squared[:, f, block], minus_half[:], start=True, stop=False)
-                nc.tensor.matmul(acc[:], c_all[:, f, block], x_of[f][:], start=False, stop=False)
+                nc.tensor.matmul(acc[:], c_all[:, f, block], x_of[f][:], start=True, stop=False)
+                nc.tensor.matmul(acc[:], c_squared[:, f, block], minus_half[:], start=False, stop=False)
                 nc.tensor.matmul(acc[:], minus_half[:, 0:P], x_squared_of[f][:], start=False, stop=True)
 
                 d2 = work.tile([P, N], F32, name=f"d2_{f}")

@@ -4,6 +4,8 @@ F, T, N = 2, 128, 512
 K, S = 256, 1024
 P = 128
 BLOCKS = K // P
+PIECE = 256
+ACC_BANKS = 6
 WARM_UP_MATMULS = 16
 
 BF16, F32, U16 = mybir.dt.bfloat16, mybir.dt.float32, mybir.dt.uint16
@@ -18,7 +20,7 @@ def tile_softkmeans_kernel(tc, x, clusters, base, offs, out):
     with (
         tc.tile_pool(name="held", bufs=1) as held,
         tc.tile_pool(name="work", bufs=2) as work,
-        tc.psum_pool(name="psum", bufs=BLOCKS * F) as psum,
+        tc.psum_pool(name="psum", bufs=ACC_BANKS) as psum,
         tc.psum_pool(name="psum_warm", bufs=1) as psum_warm,
     ):
         zeros = held.tile([P, P], BF16, name="zeros")
@@ -48,21 +50,21 @@ def tile_softkmeans_kernel(tc, x, clusters, base, offs, out):
 
         for b in range(BLOCKS):
             block = slice(b * P, (b + 1) * P)
-            root_of = []
+            root_of = [work.tile([P, N], F32, name=f"root{f}") for f in range(F)]
             for f in range(F):
-                acc = psum.tile([P, N], F32, name="acc")
-                nc.tensor.matmul(acc[:], c_all[:, f, block], x_of[f][:], start=True, stop=False)
-                nc.tensor.matmul(acc[:], c_squared[:, f, block], minus_half[:], start=False, stop=False)
-                nc.tensor.matmul(acc[:], minus_half[:, 0:P], x_squared_of[f][:], start=False, stop=True)
+                d2 = work.tile([P, N], F32, name="d2")
+                for first in range(0, N, PIECE):
+                    piece = slice(first, first + PIECE)
+                    acc = psum.tile([P, PIECE], F32, name="acc")
+                    nc.tensor.matmul(acc[:], c_all[:, f, block], x_of[f][:, piece], start=True, stop=False)
+                    nc.tensor.matmul(acc[:], c_squared[:, f, block], minus_half[:, piece], start=False, stop=False)
+                    nc.tensor.matmul(acc[:], minus_half[:, 0:P], x_squared_of[f][:, piece], start=False, stop=True)
 
-                d2 = work.tile([P, N], F32, name=f"d2_{f}")
-                if b == 0:
-                    nc.vector.tensor_scalar(d2[:], acc[:], -2.0, 0.0, ALU.mult, ALU.max)
-                else:
-                    nc.scalar.activation(d2[:], acc[:], ACT.Relu, scale=-2.0)
-                root = work.tile([P, N], F32, name=f"root{f}")
-                nc.scalar.activation(root[:], d2[:], ACT.Sqrt)
-                root_of.append(root)
+                    if b == 0:
+                        nc.vector.tensor_scalar(d2[:, piece], acc[:], -2.0, 0.0, ALU.mult, ALU.max)
+                    else:
+                        nc.scalar.activation(d2[:, piece], acc[:], ACT.Relu, scale=-2.0)
+                    nc.scalar.activation(root_of[f][:, piece], d2[:, piece], ACT.Sqrt)
 
             nc.vector.tensor_tensor(
                 window_of[b][:].indirect(offsets[:]), root_of[0][:], root_of[1][:], ALU.add

@@ -21,11 +21,11 @@ def tile_softkmeans_kernel(tc, x, clusters, base, offs, out):
         tc.tile_pool(name="held", bufs=1) as held,
         tc.tile_pool(name="work", bufs=2) as work,
         tc.psum_pool(name="psum", bufs=ACC_BANKS) as psum,
-        tc.psum_pool(name="psum_warm", bufs=1) as psum_warm,
+        tc.psum_pool(name="psum_held", bufs=1) as psum_held,
     ):
         zeros = held.tile([P, P], BF16, name="zeros")
         nc.gpsimd.memset(zeros[:], 0.0)
-        warm_up = psum_warm.tile([P, P], F32, name="warm_up")
+        warm_up = psum_held.tile([P, P], F32, name="warm_up")
         for i in range(WARM_UP_MATMULS):
             nc.tensor.matmul(warm_up[:], zeros[:], zeros[:], start=True, stop=True)
 
@@ -40,31 +40,47 @@ def tile_softkmeans_kernel(tc, x, clusters, base, offs, out):
         for b in range(BLOCKS):
             nc.sync.dma_start(window_of[b][:], base[b * P : (b + 1) * P, :])
 
-        minus_half = held.tile([T, N], BF16, name="minus_half")
+        minus_half = held.tile([T, P], BF16, name="minus_half")
         nc.vector.memset(minus_half[:], -0.5)
+        plus_half = held.tile([T, 1], BF16, name="plus_half")
+        nc.vector.memset(plus_half[:], 0.5)
         c_squared = held.tile([T, F, K], BF16, name="c_squared")
         nc.vector.tensor_mul(c_squared[:], c_all[:], c_all[:])
         x_squared_of = [held.tile([T, N], BF16, name=f"x_squared{f}") for f in range(F)]
         for f in range(F):
             nc.vector.tensor_mul(x_squared_of[f][:], x_of[f][:], x_of[f][:])
 
+        half_c2_psum = psum_held.tile([P, BLOCKS * F], F32, name="half_c2_psum")
+        for b in range(BLOCKS):
+            for f in range(F):
+                nc.tensor.matmul(
+                    half_c2_psum[:, b * F + f : b * F + f + 1],
+                    c_squared[:, f, b * P : (b + 1) * P],
+                    plus_half[:],
+                    start=True,
+                    stop=True,
+                )
+        half_c2 = held.tile([P, BLOCKS * F], F32, name="half_c2")
+        nc.vector.tensor_copy(half_c2[:], half_c2_psum[:])
+
         for b in range(BLOCKS):
             block = slice(b * P, (b + 1) * P)
             root_of = [work.tile([P, N], F32, name=f"root{f}") for f in range(F)]
             for f in range(F):
-                d2 = work.tile([P, N], F32, name="d2")
+                clipped = work.tile([P, N], F32, name="clipped")
                 for first in range(0, N, PIECE):
                     piece = slice(first, first + PIECE)
                     acc = psum.tile([P, PIECE], F32, name="acc")
-                    nc.tensor.matmul(acc[:], c_all[:, f, block], x_of[f][:, piece], start=True, stop=False)
-                    nc.tensor.matmul(acc[:], c_squared[:, f, block], minus_half[:, piece], start=False, stop=False)
-                    nc.tensor.matmul(acc[:], minus_half[:, 0:P], x_squared_of[f][:, piece], start=False, stop=True)
+                    nc.tensor.matmul(acc[:], minus_half[:], x_squared_of[f][:, piece], start=True, stop=False)
+                    nc.tensor.matmul(acc[:], c_all[:, f, block], x_of[f][:, piece], start=False, stop=True)
 
+                    this_half_c2 = half_c2[:, b * F + f : b * F + f + 1]
                     if b == 0:
-                        nc.vector.tensor_scalar(d2[:, piece], acc[:], -2.0, 0.0, ALU.mult, ALU.max)
+                        nc.vector.tensor_scalar(clipped[:, piece], acc[:], this_half_c2, 0.0, ALU.subtract, ALU.min)
+                        nc.scalar.activation(root_of[f][:, piece], clipped[:, piece], ACT.Sqrt, scale=-2.0)
                     else:
-                        nc.scalar.activation(d2[:, piece], acc[:], ACT.Relu, scale=-2.0)
-                    nc.scalar.activation(root_of[f][:, piece], d2[:, piece], ACT.Sqrt)
+                        nc.scalar.activation(clipped[:, piece], acc[:], ACT.Relu, bias=this_half_c2, scale=-1.0)
+                        nc.scalar.activation(root_of[f][:, piece], clipped[:, piece], ACT.Sqrt, scale=2.0)
 
             nc.vector.tensor_tensor(
                 window_of[b][:].indirect(offsets[:]), root_of[0][:], root_of[1][:], ALU.add

@@ -4,7 +4,7 @@ F, T, N = 2, 128, 512
 K, S = 256, 1024
 P = 128
 BLOCKS = K // P
-PIECE = 256
+PIECE = 128
 ACC_BANKS = 6
 WARM_UP_MATMULS = 16
 

@@ -23,11 +23,11 @@ def tile_softkmeans_kernel(tc, x, clusters, base, offs, out):
         tc.psum_pool(name="psum", bufs=ACC_BANKS) as psum,
         tc.psum_pool(name="psum_held", bufs=1) as psum_held,
     ):
-        zeros = held.tile([P, P], BF16, name="zeros")
-        nc.gpsimd.memset(zeros[:], 0.0)
+        minus_half = held.tile([T, P], BF16, name="minus_half")
+        nc.vector.memset(minus_half[:], -0.5)
         warm_up = psum_held.tile([P, P], F32, name="warm_up")
         for i in range(WARM_UP_MATMULS):
-            nc.tensor.matmul(warm_up[:], zeros[:], zeros[:], start=True, stop=True)
+            nc.tensor.matmul(warm_up[:], minus_half[:], minus_half[:], start=True, stop=True)
 
         c_all = held.tile([T, F, K], BF16, name="c_all")
         nc.sync.dma_start(c_all[:], clusters.rearrange("f t k -> t f k"))
@@ -40,8 +40,6 @@ def tile_softkmeans_kernel(tc, x, clusters, base, offs, out):
         for b in range(BLOCKS):
             nc.sync.dma_start(window_of[b][:], base[b * P : (b + 1) * P, :])
 
-        minus_half = held.tile([T, P], BF16, name="minus_half")
-        nc.vector.memset(minus_half[:], -0.5)
         plus_half = held.tile([T, 1], BF16, name="plus_half")
         nc.vector.memset(plus_half[:], 0.5)
         c_squared = held.tile([T, F, K], BF16, name="c_squared")

import concourse.mybir as mybir

F, T, N = 2, 128, 512
K, S = 256, 1024
P = 128
BLOCKS = K // P
PIECE = 128
ACC_BANKS = 6
WARM_UP_MATMULS = 16

BF16, F32, U16 = mybir.dt.bfloat16, mybir.dt.float32, mybir.dt.uint16
ALU = mybir.AluOpType
ACT = mybir.ActivationFunctionType

FLOPS = 2 * F * T * K * N


def tile_softkmeans_kernel(tc, x, clusters, base, offs, out):
    nc = tc.nc
    with (
        tc.tile_pool(name="held", bufs=1) as held,
        tc.tile_pool(name="work", bufs=2) as work,
        tc.psum_pool(name="psum", bufs=ACC_BANKS) as psum,
        tc.psum_pool(name="psum_held", bufs=1) as psum_held,
    ):
        minus_half = held.tile([T, P], BF16, name="minus_half")
        nc.vector.memset(minus_half[:], -0.5)
        warm_up = psum_held.tile([P, P], F32, name="warm_up")
        for i in range(WARM_UP_MATMULS):
            nc.tensor.matmul(warm_up[:], minus_half[:], minus_half[:], start=True, stop=True)

        c_all = held.tile([T, F, K], BF16, name="c_all")
        nc.sync.dma_start(c_all[:], clusters.rearrange("f t k -> t f k"))
        x_of = [held.tile([T, N], BF16, name=f"x{f}") for f in range(F)]
        for f in range(F):
            nc.sync.dma_start(x_of[f][:], x[f])
        offsets = held.tile([P, N // 16], U16, name="offsets")
        nc.sync.dma_start(offsets[:], offs)
        window_of = [held.tile([P, S], F32, name=f"window{b}") for b in range(BLOCKS)]
        for b in range(BLOCKS):
            nc.sync.dma_start(window_of[b][:], base[b * P : (b + 1) * P, :])

        plus_half = held.tile([T, 1], BF16, name="plus_half")
        nc.vector.memset(plus_half[:], 0.5)
        c_squared = held.tile([T, F, K], BF16, name="c_squared")
        nc.vector.tensor_mul(c_squared[:], c_all[:], c_all[:])
        x_squared_of = [held.tile([T, N], BF16, name=f"x_squared{f}") for f in range(F)]
        for f in range(F):
            nc.vector.tensor_mul(x_squared_of[f][:], x_of[f][:], x_of[f][:])

        half_c2_psum = psum_held.tile([P, BLOCKS * F], F32, name="half_c2_psum")
        for b in range(BLOCKS):
            for f in range(F):
                nc.tensor.matmul(
                    half_c2_psum[:, b * F + f : b * F + f + 1],
                    c_squared[:, f, b * P : (b + 1) * P],
                    plus_half[:],
                    start=True,
                    stop=True,
                )
        half_c2 = held.tile([P, BLOCKS * F], F32, name="half_c2")
        nc.vector.tensor_copy(half_c2[:], half_c2_psum[:])

        for b in range(BLOCKS):
            block = slice(b * P, (b + 1) * P)
            root_of = [work.tile([P, N], F32, name=f"root{f}") for f in range(F)]
            for f in range(F):
                clipped = work.tile([P, N], F32, name="clipped")
                for first in range(0, N, PIECE):
                    piece = slice(first, first + PIECE)
                    acc = psum.tile([P, PIECE], F32, name="acc")
                    nc.tensor.matmul(acc[:], minus_half[:], x_squared_of[f][:, piece], start=True, stop=False)
                    nc.tensor.matmul(acc[:], c_all[:, f, block], x_of[f][:, piece], start=False, stop=True)

                    this_half_c2 = half_c2[:, b * F + f : b * F + f + 1]
                    if b == 0:
                        nc.vector.tensor_scalar(clipped[:, piece], acc[:], this_half_c2, 0.0, ALU.subtract, ALU.min)
                        nc.scalar.activation(root_of[f][:, piece], clipped[:, piece], ACT.Sqrt, scale=-2.0)
                    else:
                        nc.scalar.activation(clipped[:, piece], acc[:], ACT.Relu, bias=this_half_c2, scale=-1.0)
                        nc.scalar.activation(root_of[f][:, piece], clipped[:, piece], ACT.Sqrt, scale=2.0)

            nc.vector.tensor_tensor(
                window_of[b][:].indirect(offsets[:]), root_of[0][:], root_of[1][:], ALU.add
            )
            nc.sync.dma_start(out[block, :], window_of[b][:])
